import numpy as np
import ml_dtypes


def mxq(x, axis, fmt="e4m3"):
    dtype, down = {"e4m3": (ml_dtypes.float8_e4m3fn, 7), "e5m2": (ml_dtypes.float8_e5m2, 14)}[fmt]
    v = np.moveaxis(np.asarray(x, np.float32).astype(ml_dtypes.bfloat16).astype(np.float64), axis, -1)
    blocks = v.reshape(v.shape[:-1] + (-1, 32))
    amax = np.abs(blocks).max(-1, keepdims=True)
    byte = np.maximum(np.where(amax > 0, np.frexp(amax)[1] - 1 + 127, 0) - down, 1)
    scale = np.exp2(byte - 127.0)
    codes = (blocks / scale).astype(np.float32).astype(dtype).astype(np.float64)
    return np.moveaxis((codes * scale).reshape(v.shape), -1, axis)


WIDE = False


def mx_kscale(k):
    if not WIDE:
        return np.ones(k)
    levels = np.array([10, -10, 5, -5, 0])
    if k % 512:
        return np.exp2(np.random.permutation(np.resize(levels, k // 32))).repeat(32)
    a = np.empty((k // 512, 16))
    for p in range(k // 512):
        a[p, :8] = np.random.permutation(np.resize(levels, 8))
        for g in range(8):
            far = levels[np.abs(levels - a[p, g]) >= 10]
            a[p, g + 8] = far[np.random.randint(len(far))]
    return np.exp2(a.ravel()).repeat(32)


BF16 = ml_dtypes.bfloat16


def bf(x):
    return np.asarray(x, np.float32).astype(BF16)


def f64(x):
    return np.asarray(x).astype(np.float64)


B, IN, M, OUT = 1024, 1024, 512, 512
F = 2 * M
EPS = 1e-12


def setup_inputs():
    s, t = mx_kscale(IN), mx_kscale(F)
    return {"x": bf(np.random.standard_normal((B, IN)) * s),
            "W1": bf(np.random.standard_normal((IN, F)) / np.sqrt(IN) / s[:, None] * t),
            "b1": bf(np.random.standard_normal(F) * 0.1 * t),
            "W2": bf(np.random.standard_normal((F, M)) / np.sqrt(F) / t[:, None]),
            "b2": bf(np.random.standard_normal(M) * 0.3)}


def reference(x, W1, b1, W2, b2):
    h = np.maximum((mxq(f64(x), 1, "e4m3") @ mxq(f64(W1), 0, "e4m3")) + f64(b1), 0.0)
    v = (mxq(h, 1, "e4m3") @ mxq(f64(W2), 0, "e4m3")) + f64(b2)
    norm = np.sqrt(np.sum(v * v, axis=-1, keepdims=True))
    return v / np.maximum(norm, EPS)

@@ -1,0 +1,391 @@
+from contextlib import ExitStack
+
+import concourse.mybir as mybir
+from concourse.masks import make_identity
+
+F32 = mybir.dt.float32
+BF16 = mybir.dt.bfloat16
+U32 = mybir.dt.uint32
+U8 = mybir.dt.uint8
+FP8X4 = mybir.dt.float8_e4m3fn_x4
+ACT = mybir.ActivationFunctionType
+ALU = mybir.AluOpType
+
+P = 128
+B, IN, F, M = 1024, 1024, 1024, 512
+FLOPS = 2 * B * IN * F + 2 * B * F * M
+EPS = 1e-12
+
+PROGRAM = [
+    ("ld_x", 0),
+    ("xt", 1, 0, 0),
+    ("xt", 0, 0, 0),
+    ("xe", 1, 0, 0, "V"),
+    ("ld_w1r", 0, 1),
+    ("ld_w1r", 0, 0),
+    ("ld_x", 1),
+    ("xe", 0, 0, 0, "S"),
+    ("w1r", 0, 0, "V", 0, 256),
+    ("w1r", 0, 1, "V", 0, 256),
+    ("xt", 0, 0, 1),
+    ("w1r", 0, 0, "S", 256, 512),
+    ("w1q", 0, 0),
+    ("w1r", 0, 1, "V", 256, 512),
+    ("xe", 0, 0, 1, "S"),
+    ("ld_small",),
+    ("xt", 1, 0, 1),
+    ("xe", 1, 0, 1, "S"),
+    ("ld_w1r", 1, 0),
+    ("xq", 0, 0),
+    ("ld_w1r", 1, 1),
+    ("sb2m",),
+    ("sb2c", "S"),
+    ("m1p", 0, 0, 0, 1, 0),
+    ("ld_x", 2),
+    ("w1q", 0, 1),
+    ("m1p", 2, 0, 0, 1, 0),
+    ("w1r", 1, 0, "V", 256, 512),
+    ("w1r", 1, 0, "S", 0, 256),
+    ("m1p", 1, 0, 0, 1, 0),
+    ("w1r", 1, 1, "S", 256, 512),
+    ("xq", 1, 0),
+    ("w1q", 1, 0),
+    ("m1p", 3, 0, 0, 1, 0),
+    ("xt", 1, 1, 0),
+    ("xe", 1, 1, 0, "S"),
+    ("w1r", 1, 1, "V", 0, 256),
+    ("xt", 0, 1, 0),
+    ("m1p", 0, 0, 1, 0, 1),
+    ("xe", 0, 1, 0, "V"),
+    ("w1q", 1, 1),
+    ("he", 0, 0, "S"),
+    ("m1p", 1, 0, 1, 0, 1),
+    ("m1p", 3, 0, 1, 0, 1),
+    ("m1p", 2, 0, 1, 0, 1),
+    ("m1p", 6, 0, 0, 1, 0),
+    ("he", 1, 0, "S"),
+    ("he", 3, 0, "V"),
+    ("ld_x", 3),
+    ("ld_w2", 1),
+    ("he", 2, 0, "S"),
+    ("xt", 0, 1, 1),
+    ("w2r", 1, "V", 256, 512),
+    ("ld_w2", 0),
+    ("xe", 0, 1, 1, "S"),
+    ("xt", 1, 1, 1),
+    ("xe", 1, 1, 1, "S"),
+    ("m1p", 4, 0, 0, 1, 0),
+    ("m1p", 7, 0, 0, 1, 0),
+    ("w2r", 0, "S", 0, 256),
+    ("w2r", 1, "V", 0, 256),
+    ("m1p", 6, 0, 1, 0, 1),
+    ("hr", 0, 0, "V", 256, 512),
+    ("m1p", 4, 0, 1, 0, 1),
+    ("he", 4, 0, "S"),
+    ("m1p", 5, 0, 0, 1, 0),
+    ("xq", 0, 1),
+    ("he", 6, 0, "V"),
+    ("xq", 1, 1),
+    ("m1p", 7, 0, 1, 0, 1),
+    ("he", 7, 0, "S"),
+    ("w2r", 0, "V", 256, 512),
+    ("m1p", 0, 1, 0, 1, 0),
+    ("hr", 0, 0, "V", 0, 256),
+    ("m1p", 5, 0, 1, 0, 1),
+    ("he", 5, 0, "S"),
+    ("w2q", 0),
+    ("m1p", 2, 1, 0, 1, 0),
+    ("m1p", 0, 1, 1, 0, 1),
+    ("hq", 0, 0),
+    ("m1p", 2, 1, 1, 0, 1),
+    ("m1p", 1, 1, 0, 1, 0),
+    ("he", 0, 1, "S"),
+    ("hr", 1, 0, "V", 0, 256),
+    ("m1p", 6, 1, 0, 1, 0),
+    ("m1p", 1, 1, 1, 0, 1),
+    ("he", 2, 1, "V"),
+    ("m1p", 3, 1, 0, 1, 0),
+    ("hr", 1, 0, "S", 256, 512),
+    ("m1p", 6, 1, 1, 0, 1),
+    ("m1p", 3, 1, 1, 0, 1),
+    ("w2q", 1),
+    ("m2p", 1, 0, 1, 0),
+    ("hq", 1, 0),
+    ("m1p", 4, 1, 0, 1, 0),
+    ("he", 1, 1, "S"),
+    ("he", 3, 1, "S"),
+    ("m1p", 5, 1, 0, 1, 0),
+    ("m1p", 4, 1, 1, 0, 1),
+    ("hr", 0, 1, "V", 0, 256),
+    ("m1p", 5, 1, 1, 0, 1),
+    ("he", 6, 1, "S"),
+    ("m2p", 1, 1, 0, 1),
+    ("m1p", 7, 1, 0, 1, 0),
+    ("hr", 0, 1, "V", 256, 512),
+    ("he", 4, 1, "S"),
+    ("va", 1),
+    ("m2p", 2, 0, 1, 0),
+    ("m1p", 7, 1, 1, 0, 1),
+    ("he", 5, 1, "S"),
+    ("he", 7, 1, "S"),
+    ("m2p", 2, 1, 0, 1),
+    ("hq", 0, 1),
+    ("va", 2),
+    ("hr", 1, 1, "V", 0, 256),
+    ("m2p", 0, 0, 1, 0),
+    ("m2p", 0, 1, 0, 1),
+    ("hr", 1, 1, "S", 256, 512),
+    ("sq", 1, 0, 1),
+    ("m2p", 3, 0, 1, 0),
+    ("va", 0),
+    ("sq", 0, 0, 0),
+    ("hq", 1, 1),
+    ("m2p", 3, 1, 0, 1),
+    ("m2p", 5, 0, 1, 0),
+    ("va", 3),
+    ("sq", 2, 1, 0),
+    ("tmax", 0, 2),
+    ("m2p", 5, 1, 0, 1),
+    ("tsqrt", 0, 2),
+    ("va", 5),
+    ("m2p", 4, 0, 1, 0),
+    ("m2p", 4, 1, 0, 1),
+    ("trec", 0, 2),
+    ("va", 4),
+    ("m2p", 6, 0, 1, 0),
+    ("sq", 3, 1, 1),
+    ("sq", 5, 2, 1),
+    ("tmax", 1, 2),
+    ("m2p", 6, 1, 0, 1),
+    ("sc", 1, "G", 0, 1, 0, 1, 2),
+    ("sc", 0, "V", 0, 0, 0, 0, 2),
+    ("m2p", 7, 0, 1, 0),
+    ("tsqrt", 1, 2),
+    ("sq", 4, 2, 0),
+    ("trec", 1, 2),
+    ("sc", 2, "S", 1, 0, 1, 0, 2),
+    ("m2p", 7, 1, 0, 1),
+    ("va", 6),
+    ("sc", 3, "G", 1, 1, 1, 1, 2),
+    ("tmax", 2, 2),
+    ("tsqrt", 2, 2),
+    ("sq", 6, 3, 0),
+    ("va", 7),
+    ("trec", 2, 2),
+    ("st", 0, 0, 2),
+    ("st", 1, 2, 2),
+    ("sc", 5, "V", 2, 1, 2, 1, 2),
+    ("sc", 4, "V", 2, 0, 2, 0, 2),
+    ("sq", 7, 3, 1),
+    ("tmax", 3, 2),
+    ("tsqrt", 3, 2),
+    ("st", 2, 4, 2),
+    ("trec", 3, 2),
+    ("sc", 6, "V", 3, 0, 3, 0, 1),
+    ("st", 3, 6, 1),
+    ("sc", 7, "V", 3, 1, 4, 0, 1),
+    ("st", 4, 7, 1),
+]
+
+
+def tile_geometricmanifoldnetwork_pa_kernel(tc, x, W1, b1, W2, b2, out):
+    nc = tc.nc
+    with ExitStack() as ctx:
+        sb = ctx.enter_context(tc.tile_pool(name="sb", bufs=1))
+        ps_t = ctx.enter_context(tc.psum_pool(name="ps_t", bufs=2))
+        ps_h = ctx.enter_context(tc.psum_pool(name="ps_h", bufs=4))
+        ps_v = ctx.enter_context(tc.psum_pool(name="ps_v", bufs=2))
+        ctx.enter_context(tc.manual_schedule())
+
+        tiles = {}
+
+        def get(key, shape, dtype):
+            if key not in tiles:
+                tiles[key] = sb.tile(shape, dtype, name=key, align_bytes=64)
+            return tiles[key]
+
+        x_v = x.rearrange("(p t) k -> p t k", t=8)
+        w2_v = W2.rearrange("(g p j) m -> p g j m", p=P, j=4)
+        out_v = out.rearrange("(p t) m -> p t m", t=8)
+
+        small = get("small", [P, 512], BF16)
+        nc.vector.memset(small[:], 0.0)
+        ones_b = get("ones_b", [P, P], BF16)
+        nc.vector.memset(ones_b[:], 1.0)
+        warm_in = get("warm_in", [P, 1], F32)
+        warm_out = get("warm_out", [P, 1], F32)
+        nc.vector.memset(warm_in[:], 1.0)
+        nc.scalar.activation(out=warm_out[:], in_=warm_in[:], func=ACT.Sqrt)
+        ident_f = get("ident_f", [P, P], F32)
+        make_identity(nc, ident_f[:])
+        ident_b = get("ident_b", [P, P], BF16)
+        nc.vector.tensor_copy(out=ident_b[:], in_=ident_f[:])
+        b1t = get("b1t", [P, 2, 4], BF16)
+        b2bc = get("b2bc", [P, M], F32)
+        junk = get("junk", [P, M], F32)
+
+        def copy_on(e, dst, src):
+            if e == "V":
+                nc.vector.tensor_copy(out=dst, in_=src)
+            else:
+                nc.scalar.copy(out=dst, in_=src)
+
+        def regroup(e, dst, src, c0, c1):
+            d = dst[:].rearrange("p (w t) -> p w t", t=4)
+            copy_on(
+                e,
+                d[:, c0:c1, :].rearrange("p (c i) t -> p c t i", i=4),
+                src[:, :, c0:c1].rearrange("p t (c i) -> p c t i", i=4),
+            )
+
+        def quantise(name, src):
+            codes = get("c_" + name, [P, 512], U32)
+            scales = get("s_" + name, [P, 512], U8)
+            nc.vector.quantize_mx(out=codes[:].bitcast(FP8X4), scales=scales[:], in_=src[:])
+
+        def mx_pass(acc, lhs_name, lcols, rhs_name, start, stop):
+            nc.tensor.matmul_mx(
+                out=acc[:],
+                lhsT=tiles["c_" + lhs_name][:, lcols].bitcast(FP8X4),
+                lhsT_scale=tiles["s_" + lhs_name][:, lcols],
+                rhs=tiles["c_" + rhs_name][:].bitcast(FP8X4),
+                rhs_scale=tiles["s_" + rhs_name][:],
+                start=(start == 1),
+                stop=(stop == 1),
+            )
+
+        def ld_small():
+            nc.sync.dma_start(out=b1t[:], in_=b1.rearrange("(g p t) -> p g t", g=2, t=4))
+            nc.sync.dma_start(out=small[0:1, 0:512], in_=b2.rearrange("(o m) -> o m", o=1))
+
+        def ld_w1r(g, u):
+            raw = get("raw1_%d" % g, [P, 4, F], BF16)
+            nc.sync.dma_start(
+                out=raw[:, 2 * u : 2 * u + 2, :],
+                in_=W1[512 * g : 512 * g + 512, :].rearrange("(q j) f -> q j f", j=4)[:, 2 * u : 2 * u + 2, :],
+            )
+
+        def ld_x(j):
+            xp = get("x_%d" % j, [P, 2, IN], BF16)
+            nc.sync.dma_start(out=xp[:], in_=x_v[:, 2 * j : 2 * j + 2, :])
+
+        def ld_w2(g):
+            raw = get("raw2_%d" % g, [P, 4, M], BF16)
+            nc.sync.dma_start(out=raw[:], in_=w2_v[:, g, :, :])
+
+        def sb2m():
+            pb2 = ps_v.tile([P, M], F32, name="pb2", tag="v")
+            tiles["pb2"] = pb2
+            nc.tensor.matmul(out=pb2[:], lhsT=ones_b[:], rhs=small[:, 0:512], start=True, stop=True)
+
+        def sb2c(e):
+            copy_on(e, b2bc[:], tiles["pb2"][:])
+
+        def w1r(g, fh, e, c0, c1):
+            src = tiles["raw1_%d" % g][:, :, 512 * fh : 512 * fh + 512]
+            dst = get("g_w1_%d%d" % (g, fh), [P, 2048], BF16)
+            m0, m1 = c0 // 4, c1 // 4
+            copy_on(
+                e,
+                dst[:].rearrange("p (t m j) -> p m j t", t=4, j=4)[:, m0:m1, :, :],
+                src.rearrange("p j (m t) -> p m j t", t=4)[:, m0:m1, :, :],
+            )
+
+        def w1q(g, fh):
+            quantise("w1_%d%d" % (g, fh), tiles["g_w1_%d%d" % (g, fh)])
+
+        def w2r(g, e, c0, c1):
+            regroup(e, get("g_w2_%d" % g, [P, 2048], BF16), tiles["raw2_%d" % g][:], c0, c1)
+
+        def w2q(g):
+            quantise("w2_%d" % g, tiles["g_w2_%d" % g])
+
+        def xt(g, bh, a):
+            pt = ps_t.tile([P, 2, 2, P], F32, name="pt", tag="t")
+            tiles["pt_%d%d%d" % (g, bh, a)] = pt
+            x_w = tiles["x_%d" % (2 * bh + a)][:].rearrange("p t k -> p (t k)").bitcast(F32)
+            for t in range(2):
+                for u in range(2):
+                    c0 = 512 * t + 256 * g
+                    nc.tensor.transpose(out=pt[:, t, u, :], in_=x_w[:, c0 + u : c0 + 256 : 2], identity=ident_f[:])
+
+        def xe(g, bh, a, e):
+            gx = get("g_x_%d%d" % (g, bh), [P, 2048], BF16)
+            dst = gx[:].bitcast(F32).rearrange("q (a t b u) -> q a t b u", a=2, t=2, u=2)[:, a, :, :, :]
+            copy_on(e, dst, tiles["pt_%d%d%d" % (g, bh, a)][:].rearrange("q t u b -> q t b u"))
+
+        def xq(g, bh):
+            quantise("x_%d%d" % (g, bh), tiles["g_x_%d%d" % (g, bh)])
+
+        def m1p(ft, bh, g, start, stop):
+            if start == 1:
+                tiles["ph_%d%d" % (ft, bh)] = ps_h.tile([P, 512], F32, name="ph", tag="h")
+            fh, r = divmod(ft, 4)
+            mx_pass(tiles["ph_%d%d" % (ft, bh)], "w1_%d%d" % (g, fh), slice(P * r, P * r + P), "x_%d%d" % (g, bh), start, stop)
+
+        def he(ft, bh, e):
+            g2, t = divmod(ft, 4)
+            ht = get("ht_%d%d" % (g2, bh), [P, 4, 512], BF16)
+            ph = tiles["ph_%d%d" % (ft, bh)]
+            if e == "V":
+                nc.vector.tensor_scalar(
+                    out=ht[:, t, :], in0=ph[:], scalar1=b1t[:, g2, t : t + 1], scalar2=0.0, op0=ALU.add, op1=ALU.max
+                )
+            else:
+                nc.scalar.activation(out=ht[:, t, :], in_=ph[:], func=ACT.Relu, bias=b1t[:, g2, t : t + 1], scale=1.0)
+
+        def hr(g2, bh, e, c0, c1):
+            regroup(e, get("g_h_%d%d" % (g2, bh), [P, 2048], BF16), tiles["ht_%d%d" % (g2, bh)][:], c0, c1)
+
+        def hq(g2, bh):
+            quantise("h_%d%d" % (g2, bh), tiles["g_h_%d%d" % (g2, bh)])
+
+        def m2p(bt, g, start, stop):
+            if start == 1:
+                tiles["pv_%d" % bt] = ps_v.tile([P, M], F32, name="pv", tag="v")
+            bh, r = divmod(bt, 4)
+            mx_pass(tiles["pv_%d" % bt], "h_%d%d" % (g, bh), slice(P * r, P * r + P), "w2_%d" % g, start, stop)
+
+        def va(bt):
+            v = get("v_%d" % bt, [P, M], F32)
+            nc.vector.tensor_tensor(out=v[:], in0=tiles["pv_%d" % bt][:], in1=b2bc[:], op=ALU.add)
+
+        def sq(bt, gid, j):
+            ss = get("ss_%d" % gid, [P, 4], F32)
+            nc.scalar.activation(out=junk[:], in_=tiles["v_%d" % bt][:], func=ACT.Square, accum_out=ss[:, j : j + 1])
+
+        def tmax(gid, n):
+            ssm = get("ssm_%d" % gid, [P, 4], F32)
+            nc.vector.tensor_scalar_max(out=ssm[:, 0:n], in0=tiles["ss_%d" % gid][:, 0:n], scalar1=EPS * EPS)
+
+        def tsqrt(gid, n):
+            nrm = get("nrm_%d" % gid, [P, 4], F32)
+            nc.scalar.activation(out=nrm[:, 0:n], in_=tiles["ssm_%d" % gid][:, 0:n], func=ACT.Sqrt)
+
+        def trec(gid, n):
+            rinv = get("rinv_%d" % gid, [P, 4], F32)
+            nc.vector.reciprocal(out=rinv[:, 0:n], in_=tiles["nrm_%d" % gid][:, 0:n])
+
+        def sc(bt, e, gid, j, sid, k, n):
+            o = get("o_%d" % sid, [P, n, M], F32)
+            r = tiles["rinv_%d" % gid][:, j : j + 1]
+            v = tiles["v_%d" % bt]
+            if e == "V":
+                nc.vector.tensor_scalar_mul(out=o[:, k, :], in0=v[:], scalar1=r)
+            elif e == "S":
+                nc.scalar.activation(out=o[:, k, :], in_=v[:], func=ACT.Copy, scale=r)
+            else:
+                nc.gpsimd.tensor_scalar(out=o[:, k, :], in0=v[:], scalar1=r, scalar2=0.0, op0=ALU.mult, op1=ALU.add)
+
+        def st(sid, bt0, n):
+            nc.sync.dma_start(out=out_v[:, bt0 : bt0 + n, :], in_=tiles["o_%d" % sid][:])
+
+        steps = {
+            "ld_small": ld_small, "ld_w1r": ld_w1r, "ld_x": ld_x, "ld_w2": ld_w2,
+            "sb2m": sb2m, "sb2c": sb2c,
+            "w1r": w1r, "w1q": w1q, "w2r": w2r, "w2q": w2q, "xt": xt, "xe": xe, "xq": xq,
+            "m1p": m1p, "he": he, "hr": hr, "hq": hq, "m2p": m2p, "va": va, "sq": sq,
+            "tmax": tmax, "tsqrt": tsqrt, "trec": trec, "sc": sc, "st": st,
+        }
+        for entry in PROGRAM:
+            steps[entry[0]](*entry[1:])

@@ -16,186 +16,18 @@ B, IN, F, M = 1024, 1024, 1024, 512
 FLOPS = 2 * B * IN * F + 2 * B * F * M
 EPS = 1e-12
 
-PROGRAM = [
-    ("ld_x", 0),
-    ("xt", 1, 0, 0),
-    ("xt", 0, 0, 0),
-    ("xe", 1, 0, 0, "V"),
-    ("ld_w1r", 0, 1),
-    ("ld_w1r", 0, 0),
-    ("ld_x", 1),
-    ("xe", 0, 0, 0, "S"),
-    ("w1r", 0, 0, "V", 0, 256),
-    ("w1r", 0, 1, "V", 0, 256),
-    ("xt", 0, 0, 1),
-    ("w1r", 0, 0, "S", 256, 512),
-    ("w1q", 0, 0),
-    ("w1r", 0, 1, "V", 256, 512),
-    ("xe", 0, 0, 1, "S"),
-    ("ld_small",),
-    ("xt", 1, 0, 1),
-    ("xe", 1, 0, 1, "S"),
-    ("ld_w1r", 1, 0),
-    ("xq", 0, 0),
-    ("ld_w1r", 1, 1),
-    ("sb2m",),
-    ("sb2c", "S"),
-    ("m1p", 0, 0, 0, 1, 0),
-    ("ld_x", 2),
-    ("w1q", 0, 1),
-    ("m1p", 2, 0, 0, 1, 0),
-    ("w1r", 1, 0, "V", 256, 512),
-    ("w1r", 1, 0, "S", 0, 256),
-    ("m1p", 1, 0, 0, 1, 0),
-    ("w1r", 1, 1, "S", 256, 512),
-    ("xq", 1, 0),
-    ("w1q", 1, 0),
-    ("m1p", 3, 0, 0, 1, 0),
-    ("xt", 1, 1, 0),
-    ("xe", 1, 1, 0, "S"),
-    ("w1r", 1, 1, "V", 0, 256),
-    ("xt", 0, 1, 0),
-    ("m1p", 0, 0, 1, 0, 1),
-    ("xe", 0, 1, 0, "V"),
-    ("w1q", 1, 1),
-    ("he", 0, 0, "S"),
-    ("m1p", 1, 0, 1, 0, 1),
-    ("m1p", 3, 0, 1, 0, 1),
-    ("m1p", 2, 0, 1, 0, 1),
-    ("m1p", 6, 0, 0, 1, 0),
-    ("he", 1, 0, "S"),
-    ("he", 3, 0, "V"),
-    ("ld_x", 3),
-    ("ld_w2", 1),
-    ("he", 2, 0, "S"),
-    ("xt", 0, 1, 1),
-    ("w2r", 1, "V", 256, 512),
-    ("ld_w2", 0),
-    ("xe", 0, 1, 1, "S"),
-    ("xt", 1, 1, 1),
-    ("xe", 1, 1, 1, "S"),
-    ("m1p", 4, 0, 0, 1, 0),
-    ("m1p", 7, 0, 0, 1, 0),
-    ("w2r", 0, "S", 0, 256),
-    ("w2r", 1, "V", 0, 256),
-    ("m1p", 6, 0, 1, 0, 1),
-    ("hr", 0, 0, "V", 256, 512),
-    ("m1p", 4, 0, 1, 0, 1),
-    ("he", 4, 0, "S"),
-    ("m1p", 5, 0, 0, 1, 0),
-    ("xq", 0, 1),
-    ("he", 6, 0, "V"),
-    ("xq", 1, 1),
-    ("m1p", 7, 0, 1, 0, 1),
-    ("he", 7, 0, "S"),
-    ("w2r", 0, "V", 256, 512),
-    ("m1p", 0, 1, 0, 1, 0),
-    ("hr", 0, 0, "V", 0, 256),
-    ("m1p", 5, 0, 1, 0, 1),
-    ("he", 5, 0, "S"),
-    ("w2q", 0),
-    ("m1p", 2, 1, 0, 1, 0),
-    ("m1p", 0, 1, 1, 0, 1),
-    ("hq", 0, 0),
-    ("m1p", 2, 1, 1, 0, 1),
-    ("m1p", 1, 1, 0, 1, 0),
-    ("he", 0, 1, "S"),
-    ("hr", 1, 0, "V", 0, 256),
-    ("m1p", 6, 1, 0, 1, 0),
-    ("m1p", 1, 1, 1, 0, 1),
-    ("he", 2, 1, "V"),
-    ("m1p", 3, 1, 0, 1, 0),
-    ("hr", 1, 0, "S", 256, 512),
-    ("m1p", 6, 1, 1, 0, 1),
-    ("m1p", 3, 1, 1, 0, 1),
-    ("w2q", 1),
-    ("m2p", 1, 0, 1, 0),
-    ("hq", 1, 0),
-    ("m1p", 4, 1, 0, 1, 0),
-    ("he", 1, 1, "S"),
-    ("he", 3, 1, "S"),
-    ("m1p", 5, 1, 0, 1, 0),
-    ("m1p", 4, 1, 1, 0, 1),
-    ("hr", 0, 1, "V", 0, 256),
-    ("m1p", 5, 1, 1, 0, 1),
-    ("he", 6, 1, "S"),
-    ("m2p", 1, 1, 0, 1),
-    ("m1p", 7, 1, 0, 1, 0),
-    ("hr", 0, 1, "V", 256, 512),
-    ("he", 4, 1, "S"),
-    ("va", 1),
-    ("m2p", 2, 0, 1, 0),
-    ("m1p", 7, 1, 1, 0, 1),
-    ("he", 5, 1, "S"),
-    ("he", 7, 1, "S"),
-    ("m2p", 2, 1, 0, 1),
-    ("hq", 0, 1),
-    ("va", 2),
-    ("hr", 1, 1, "V", 0, 256),
-    ("m2p", 0, 0, 1, 0),
-    ("m2p", 0, 1, 0, 1),
-    ("hr", 1, 1, "S", 256, 512),
-    ("sq", 1, 0, 1),
-    ("m2p", 3, 0, 1, 0),
-    ("va", 0),
-    ("sq", 0, 0, 0),
-    ("hq", 1, 1),
-    ("m2p", 3, 1, 0, 1),
-    ("m2p", 5, 0, 1, 0),
-    ("va", 3),
-    ("sq", 2, 1, 0),
-    ("tmax", 0, 2),
-    ("m2p", 5, 1, 0, 1),
-    ("tsqrt", 0, 2),
-    ("va", 5),
-    ("m2p", 4, 0, 1, 0),
-    ("m2p", 4, 1, 0, 1),
-    ("trec", 0, 2),
-    ("va", 4),
-    ("m2p", 6, 0, 1, 0),
-    ("sq", 3, 1, 1),
-    ("sq", 5, 2, 1),
-    ("tmax", 1, 2),
-    ("m2p", 6, 1, 0, 1),
-    ("sc", 1, "G", 0, 1, 0, 1, 2),
-    ("sc", 0, "V", 0, 0, 0, 0, 2),
-    ("m2p", 7, 0, 1, 0),
-    ("tsqrt", 1, 2),
-    ("sq", 4, 2, 0),
-    ("trec", 1, 2),
-    ("sc", 2, "S", 1, 0, 1, 0, 2),
-    ("m2p", 7, 1, 0, 1),
-    ("va", 6),
-    ("sc", 3, "G", 1, 1, 1, 1, 2),
-    ("tmax", 2, 2),
-    ("tsqrt", 2, 2),
-    ("sq", 6, 3, 0),
-    ("va", 7),
-    ("trec", 2, 2),
-    ("st", 0, 0, 2),
-    ("st", 1, 2, 2),
-    ("sc", 5, "V", 2, 1, 2, 1, 2),
-    ("sc", 4, "V", 2, 0, 2, 0, 2),
-    ("sq", 7, 3, 1),
-    ("tmax", 3, 2),
-    ("tsqrt", 3, 2),
-    ("st", 2, 4, 2),
-    ("trec", 3, 2),
-    ("sc", 6, "V", 3, 0, 3, 0, 1),
-    ("st", 3, 6, 1),
-    ("sc", 7, "V", 3, 1, 4, 0, 1),
-    ("st", 4, 7, 1),
-]
-
 
 def tile_geometricmanifoldnetwork_pa_kernel(tc, x, W1, b1, W2, b2, out):
     nc = tc.nc
     with ExitStack() as ctx:
         sb = ctx.enter_context(tc.tile_pool(name="sb", bufs=1))
-        ps_t = ctx.enter_context(tc.psum_pool(name="ps_t", bufs=2))
-        ps_h = ctx.enter_context(tc.psum_pool(name="ps_h", bufs=4))
-        ps_v = ctx.enter_context(tc.psum_pool(name="ps_v", bufs=2))
+        ps = ctx.enter_context(tc.psum_pool(name="ps", bufs=8))
         ctx.enter_context(tc.manual_schedule())
+
+        x_v = x.rearrange("(p r) k -> p r k", r=8)
+        out_v = out.rearrange("(p r) m -> p r m", r=8)
+        w1_v = W1.rearrange("(g p j) f -> g p j f", g=2, j=4)
+        w2_v = W2.rearrange("(g p j) m -> g p j m", g=2, j=4)
 
         tiles = {}
 
@@ -204,25 +36,23 @@ def tile_geometricmanifoldnetwork_pa_kernel(tc, x, W1, b1, W2, b2, out):
                 tiles[key] = sb.tile(shape, dtype, name=key, align_bytes=64)
             return tiles[key]
 
-        x_v = x.rearrange("(p t) k -> p t k", t=8)
-        w2_v = W2.rearrange("(g p j) m -> p g j m", p=P, j=4)
-        out_v = out.rearrange("(p t) m -> p t m", t=8)
+        def bank(key, shape, dtype):
+            tiles[key] = ps.tile(shape, dtype, name="bank", tag="bank")
+            return tiles[key]
 
-        small = get("small", [P, 512], BF16)
-        nc.vector.memset(small[:], 0.0)
+        b2row = get("b2row", [P, M], BF16)
+        nc.vector.memset(b2row[:], 0.0)
         ones_b = get("ones_b", [P, P], BF16)
         nc.vector.memset(ones_b[:], 1.0)
-        warm_in = get("warm_in", [P, 1], F32)
-        warm_out = get("warm_out", [P, 1], F32)
-        nc.vector.memset(warm_in[:], 1.0)
-        nc.scalar.activation(out=warm_out[:], in_=warm_in[:], func=ACT.Sqrt)
+        warm = get("warm", [P, 2], F32)
+        nc.vector.memset(warm[:], 1.0)
+        nc.scalar.activation(out=warm[:, 1:2], in_=warm[:, 0:1], func=ACT.Abs_reciprocal_sqrt)
         ident_f = get("ident_f", [P, P], F32)
         make_identity(nc, ident_f[:])
         ident_b = get("ident_b", [P, P], BF16)
         nc.vector.tensor_copy(out=ident_b[:], in_=ident_f[:])
         b1t = get("b1t", [P, 2, 4], BF16)
         b2bc = get("b2bc", [P, M], F32)
-        junk = get("junk", [P, M], F32)
 
         def copy_on(e, dst, src):
             if e == "V":
@@ -230,162 +60,315 @@ def tile_geometricmanifoldnetwork_pa_kernel(tc, x, W1, b1, W2, b2, out):
             else:
                 nc.scalar.copy(out=dst, in_=src)
 
-        def regroup(e, dst, src, c0, c1):
-            d = dst[:].rearrange("p (w t) -> p w t", t=4)
-            copy_on(
-                e,
-                d[:, c0:c1, :].rearrange("p (c i) t -> p c t i", i=4),
-                src[:, :, c0:c1].rearrange("p t (c i) -> p c t i", i=4),
-            )
-
         def quantise(name, src):
             codes = get("c_" + name, [P, 512], U32)
             scales = get("s_" + name, [P, 512], U8)
-            nc.vector.quantize_mx(out=codes[:].bitcast(FP8X4), scales=scales[:], in_=src[:])
+            nc.vector.quantize_mx(out=codes[:].bitcast(FP8X4), scales=scales[:], in_=src)
 
-        def mx_pass(acc, lhs_name, lcols, rhs_name, start, stop):
+        def mx_pass(acc, lhs_name, r, rhs_name, start, stop):
+            cols = slice(P * r, P * r + P)
             nc.tensor.matmul_mx(
                 out=acc[:],
-                lhsT=tiles["c_" + lhs_name][:, lcols].bitcast(FP8X4),
-                lhsT_scale=tiles["s_" + lhs_name][:, lcols],
+                lhsT=tiles["c_" + lhs_name][:, cols].bitcast(FP8X4),
+                lhsT_scale=tiles["s_" + lhs_name][:, cols],
                 rhs=tiles["c_" + rhs_name][:].bitcast(FP8X4),
                 rhs_scale=tiles["s_" + rhs_name][:],
-                start=(start == 1),
-                stop=(stop == 1),
+                start=start,
+                stop=stop,
             )
 
-        def ld_small():
-            nc.sync.dma_start(out=b1t[:], in_=b1.rearrange("(g p t) -> p g t", g=2, t=4))
-            nc.sync.dma_start(out=small[0:1, 0:512], in_=b2.rearrange("(o m) -> o m", o=1))
+        def ld_x(r, n):
+            xp = get("x_%d" % r, [P, n, IN], BF16)
+            for i in range(n):
+                tiles["xr_%d" % (r + i)] = xp[:, i, :]
+            nc.sync.dma_start(out=xp[:], in_=x_v[:, r : r + n, :])
 
-        def ld_w1r(g, u):
-            raw = get("raw1_%d" % g, [P, 4, F], BF16)
-            nc.sync.dma_start(
-                out=raw[:, 2 * u : 2 * u + 2, :],
-                in_=W1[512 * g : 512 * g + 512, :].rearrange("(q j) f -> q j f", j=4)[:, 2 * u : 2 * u + 2, :],
-            )
-
-        def ld_x(j):
-            xp = get("x_%d" % j, [P, 2, IN], BF16)
-            nc.sync.dma_start(out=xp[:], in_=x_v[:, 2 * j : 2 * j + 2, :])
+        def ld_w1(g, fh):
+            raw = get("raw1_%d%d" % (g, fh), [P, 4, 512], BF16)
+            nc.sync.dma_start(out=raw[:], in_=w1_v[g, :, :, 512 * fh : 512 * fh + 512])
 
         def ld_w2(g):
             raw = get("raw2_%d" % g, [P, 4, M], BF16)
-            nc.sync.dma_start(out=raw[:], in_=w2_v[:, g, :, :])
+            nc.sync.dma_start(out=raw[:], in_=w2_v[g])
 
-        def sb2m():
-            pb2 = ps_v.tile([P, M], F32, name="pb2", tag="v")
-            tiles["pb2"] = pb2
-            nc.tensor.matmul(out=pb2[:], lhsT=ones_b[:], rhs=small[:, 0:512], start=True, stop=True)
+        def ld_b():
+            nc.sync.dma_start(out=b1t[:], in_=b1.rearrange("(g p t) -> p g t", g=2, t=4))
+            nc.sync.dma_start(out=b2row[0:1, :], in_=b2.rearrange("(o m) -> o m", o=1))
 
-        def sb2c(e):
+        def b2_spread():
+            pb2 = bank("pb2", [P, M], F32)
+            nc.tensor.matmul(out=pb2[:], lhsT=ones_b[:], rhs=b2row[:], start=True, stop=True)
+
+        def b2_copy(e):
             copy_on(e, b2bc[:], tiles["pb2"][:])
 
-        def w1r(g, fh, e, c0, c1):
-            src = tiles["raw1_%d" % g][:, :, 512 * fh : 512 * fh + 512]
-            dst = get("g_w1_%d%d" % (g, fh), [P, 2048], BF16)
-            m0, m1 = c0 // 4, c1 // 4
-            copy_on(
-                e,
-                dst[:].rearrange("p (t m j) -> p m j t", t=4, j=4)[:, m0:m1, :, :],
-                src.rearrange("p j (m t) -> p m j t", t=4)[:, m0:m1, :, :],
-            )
-
-        def w1q(g, fh):
-            quantise("w1_%d%d" % (g, fh), tiles["g_w1_%d%d" % (g, fh)])
-
-        def w2r(g, e, c0, c1):
-            regroup(e, get("g_w2_%d" % g, [P, 2048], BF16), tiles["raw2_%d" % g][:], c0, c1)
-
-        def w2q(g):
-            quantise("w2_%d" % g, tiles["g_w2_%d" % g])
-
-        def xt(g, bh, a):
-            pt = ps_t.tile([P, 2, 2, P], F32, name="pt", tag="t")
-            tiles["pt_%d%d%d" % (g, bh, a)] = pt
-            x_w = tiles["x_%d" % (2 * bh + a)][:].rearrange("p t k -> p (t k)").bitcast(F32)
-            for t in range(2):
+        def xt(r):
+            pt = bank("pt_%d" % r, [P, 2, 2, P], F32)
+            words = tiles["xr_%d" % r].bitcast(F32)
+            for g in range(2):
                 for u in range(2):
-                    c0 = 512 * t + 256 * g
-                    nc.tensor.transpose(out=pt[:, t, u, :], in_=x_w[:, c0 + u : c0 + 256 : 2], identity=ident_f[:])
+                    c0 = 256 * g
+                    nc.tensor.transpose(out=pt[:, g, u, :], in_=words[:, c0 + u : c0 + 256 : 2], identity=ident_f[:])
 
-        def xe(g, bh, a, e):
-            gx = get("g_x_%d%d" % (g, bh), [P, 2048], BF16)
-            dst = gx[:].bitcast(F32).rearrange("q (a t b u) -> q a t b u", a=2, t=2, u=2)[:, a, :, :, :]
-            copy_on(e, dst, tiles["pt_%d%d%d" % (g, bh, a)][:].rearrange("q t u b -> q t b u"))
+        def xe(r, e):
+            bh, i = divmod(r, 4)
+            gx = get("g_x_%d" % bh, [P, 4096], BF16)
+            dst = gx[:].bitcast(F32).rearrange("p (g i b u) -> p i g b u", g=2, i=4, u=2)[:, i, :, :, :]
+            copy_on(e, dst, tiles["pt_%d" % r][:].rearrange("p g u b -> p g b u"))
 
         def xq(g, bh):
-            quantise("x_%d%d" % (g, bh), tiles["g_x_%d%d" % (g, bh)])
+            quantise("x_%d%d" % (g, bh), tiles["g_x_%d" % bh][:, 2048 * g : 2048 * g + 2048])
 
-        def m1p(ft, bh, g, start, stop):
-            if start == 1:
-                tiles["ph_%d%d" % (ft, bh)] = ps_h.tile([P, 512], F32, name="ph", tag="h")
-            fh, r = divmod(ft, 4)
-            mx_pass(tiles["ph_%d%d" % (ft, bh)], "w1_%d%d" % (g, fh), slice(P * r, P * r + P), "x_%d%d" % (g, bh), start, stop)
+        def w1_tile(g, fh):
+            return get("g_w1_%d%d" % (g, fh), [P, 2048], BF16)
 
-        def he(ft, bh, e):
-            g2, t = divmod(ft, 4)
-            ht = get("ht_%d%d" % (g2, bh), [P, 4, 512], BF16)
-            ph = tiles["ph_%d%d" % (ft, bh)]
+        def w1r(g, fh, h, e):
+            ms = slice(64 * h, 64 * h + 64)
+            copy_on(
+                e,
+                w1_tile(g, fh)[:].rearrange("p (t m j) -> p m j t", t=4, j=4)[:, ms, :, :],
+                tiles["raw1_%d%d" % (g, fh)][:].rearrange("p j (m t) -> p m j t", t=4)[:, ms, :, :],
+            )
+
+        def w1s(g, fh, h):
+            pw = bank("pw1_%d%d%d" % (g, fh, h), [P, 2, 512], BF16)
+            src = tiles["raw1_%d%d" % (g, fh)][:].rearrange("p j (m t) -> p t m j", t=4)
+            for i in range(2):
+                nc.tensor.matmul(out=pw[:, i, :], lhsT=ident_b[:], rhs=src[:, 2 * h + i, :, :], start=True, stop=True)
+
+        def w1e(g, fh, h, e):
+            pw = tiles["pw1_%d%d%d" % (g, fh, h)]
+            dst = w1_tile(g, fh)[:, 1024 * h : 1024 * h + 1024].bitcast(F32)
+            copy_on(e, dst, pw[:].rearrange("p i c -> p (i c)").bitcast(F32))
+
+        def w1q(g, fh):
+            quantise("w1_%d%d" % (g, fh), w1_tile(g, fh)[:])
+
+        def w2_tile(g):
+            return get("g_w2_%d" % g, [P, 2048], BF16)
+
+        def regroup(e, dst, src, h):
+            c0 = 256 * h
+            copy_on(
+                e,
+                dst[:, 4 * c0 : 4 * c0 + 1024].rearrange("p (c i t) -> p c t i", i=4, t=4),
+                src[:, :, c0 : c0 + 256].rearrange("p t (c i) -> p c t i", i=4),
+            )
+
+        def w2r(g, h, e):
+            regroup(e, w2_tile(g), tiles["raw2_%d" % g], h)
+
+        def w2s(g, h):
+            pw = bank("pw2_%d%d" % (g, h), [P, 2, 512], BF16)
+            src = tiles["raw2_%d" % g][:].rearrange("p j c -> p c j")
+            for i in range(2):
+                c0 = 256 * h + 128 * i
+                nc.tensor.matmul(out=pw[:, i, :], lhsT=ident_b[:], rhs=src[:, c0 : c0 + 128, :], start=True, stop=True)
+
+        def w2e(g, h, e):
+            dst = w2_tile(g)[:, 1024 * h : 1024 * h + 1024].bitcast(F32)
+            copy_on(e, dst, tiles["pw2_%d%d" % (g, h)][:].rearrange("p i c -> p (i c)").bitcast(F32))
+
+        def w2q(g):
+            quantise("w2_%d" % g, w2_tile(g)[:])
+
+        def m1(fh, t, bh, g):
+            key = "ph_%d%d%d" % (fh, t, bh)
+            if g == 0:
+                bank(key, [P, 512], F32)
+            mx_pass(tiles[key], "w1_%d%d" % (g, fh), t, "x_%d%d" % (g, bh), g == 0, g == 1)
+
+        def he(fh, t, bh, e):
+            ht = get("ht_%d%d" % (fh, bh), [P, 4, 512], BF16)
+            ph = tiles["ph_%d%d%d" % (fh, t, bh)]
+            bias = b1t[:, fh, t : t + 1]
             if e == "V":
                 nc.vector.tensor_scalar(
-                    out=ht[:, t, :], in0=ph[:], scalar1=b1t[:, g2, t : t + 1], scalar2=0.0, op0=ALU.add, op1=ALU.max
+                    out=ht[:, t, :], in0=ph[:], scalar1=bias, scalar2=0.0, op0=ALU.add, op1=ALU.max
                 )
             else:
-                nc.scalar.activation(out=ht[:, t, :], in_=ph[:], func=ACT.Relu, bias=b1t[:, g2, t : t + 1], scale=1.0)
+                nc.scalar.activation(out=ht[:, t, :], in_=ph[:], func=ACT.Relu, bias=bias, scale=1.0)
 
-        def hr(g2, bh, e, c0, c1):
-            regroup(e, get("g_h_%d%d" % (g2, bh), [P, 2048], BF16), tiles["ht_%d%d" % (g2, bh)][:], c0, c1)
+        def hr(fh, bh, h, e):
+            regroup(e, get("g_h_%d%d" % (fh, bh), [P, 2048], BF16), tiles["ht_%d%d" % (fh, bh)], h)
 
-        def hq(g2, bh):
-            quantise("h_%d%d" % (g2, bh), tiles["g_h_%d%d" % (g2, bh)])
+        def hq(fh, bh):
+            quantise("h_%d%d" % (fh, bh), tiles["g_h_%d%d" % (fh, bh)][:])
 
-        def m2p(bt, g, start, stop):
-            if start == 1:
-                tiles["pv_%d" % bt] = ps_v.tile([P, M], F32, name="pv", tag="v")
-            bh, r = divmod(bt, 4)
-            mx_pass(tiles["pv_%d" % bt], "h_%d%d" % (g, bh), slice(P * r, P * r + P), "w2_%d" % g, start, stop)
+        def m2(r, g):
+            key = "pv_%d" % r
+            if g == 0:
+                bank(key, [P, M], F32)
+            bh, i = divmod(r, 4)
+            mx_pass(tiles[key], "h_%d%d" % (g, bh), i, "w2_%d" % g, g == 0, g == 1)
 
-        def va(bt):
-            v = get("v_%d" % bt, [P, M], F32)
-            nc.vector.tensor_tensor(out=v[:], in0=tiles["pv_%d" % bt][:], in1=b2bc[:], op=ALU.add)
+        def va(r):
+            v = get("v_%d" % r, [P, M], F32)
+            nc.vector.tensor_tensor(out=v[:], in0=tiles["pv_%d" % r][:], in1=b2bc[:], op=ALU.add)
 
-        def sq(bt, gid, j):
-            ss = get("ss_%d" % gid, [P, 4], F32)
-            nc.scalar.activation(out=junk[:], in_=tiles["v_%d" % bt][:], func=ACT.Square, accum_out=ss[:, j : j + 1])
+        def sq(r):
+            ss = get("ss_%d" % (r // 2), [P, 2], F32)
+            junk = get("junk_%d" % (r % 2), [P, M], F32)
+            i = r % 2
+            nc.scalar.activation(out=junk[:], in_=tiles["v_%d" % r][:], func=ACT.Square, accum_out=ss[:, i : i + 1])
 
-        def tmax(gid, n):
-            ssm = get("ssm_%d" % gid, [P, 4], F32)
-            nc.vector.tensor_scalar_max(out=ssm[:, 0:n], in0=tiles["ss_%d" % gid][:, 0:n], scalar1=EPS * EPS)
+        def norm(r, n):
+            u, i = divmod(r, 2)
+            ss = tiles["ss_%d" % u]
+            over = get("over_%d" % u, [P, 2], F32)
+            rinv = get("rinv_%d" % u, [P, 2], F32)
+            c = slice(i, i + n)
+            nc.scalar.activation(out=over[:, c], in_=ss[:, c], func=ACT.Relu, bias=-EPS * EPS)
+            nc.scalar.activation(out=rinv[:, c], in_=over[:, c], func=ACT.Abs_reciprocal_sqrt, bias=EPS * EPS)
 
-        def tsqrt(gid, n):
-            nrm = get("nrm_%d" % gid, [P, 4], F32)
-            nc.scalar.activation(out=nrm[:, 0:n], in_=tiles["ssm_%d" % gid][:, 0:n], func=ACT.Sqrt)
-
-        def trec(gid, n):
-            rinv = get("rinv_%d" % gid, [P, 4], F32)
-            nc.vector.reciprocal(out=rinv[:, 0:n], in_=tiles["nrm_%d" % gid][:, 0:n])
-
-        def sc(bt, e, gid, j, sid, k, n):
-            o = get("o_%d" % sid, [P, n, M], F32)
-            r = tiles["rinv_%d" % gid][:, j : j + 1]
-            v = tiles["v_%d" % bt]
+        def sc(r, e):
+            o = get("o_%d" % (r // 2), [P, 2, M], F32)
+            i = r % 2
+            rinv = tiles["rinv_%d" % (r // 2)][:, i : i + 1]
+            v = tiles["v_%d" % r]
             if e == "V":
-                nc.vector.tensor_scalar_mul(out=o[:, k, :], in0=v[:], scalar1=r)
-            elif e == "S":
-                nc.scalar.activation(out=o[:, k, :], in_=v[:], func=ACT.Copy, scale=r)
+                nc.vector.tensor_scalar_mul(out=o[:, i, :], in0=v[:], scalar1=rinv)
             else:
-                nc.gpsimd.tensor_scalar(out=o[:, k, :], in0=v[:], scalar1=r, scalar2=0.0, op0=ALU.mult, op1=ALU.add)
+                nc.scalar.activation(out=o[:, i, :], in_=v[:], func=ACT.Copy, scale=rinv)
 
-        def st(sid, bt0, n):
-            nc.sync.dma_start(out=out_v[:, bt0 : bt0 + n, :], in_=tiles["o_%d" % sid][:])
+        def st(r, n):
+            i = r % 2
+            nc.sync.dma_start(out=out_v[:, r : r + n, :], in_=tiles["o_%d" % (r // 2)][:, i : i + n, :])
 
-        steps = {
-            "ld_small": ld_small, "ld_w1r": ld_w1r, "ld_x": ld_x, "ld_w2": ld_w2,
-            "sb2m": sb2m, "sb2c": sb2c,
-            "w1r": w1r, "w1q": w1q, "w2r": w2r, "w2q": w2q, "xt": xt, "xe": xe, "xq": xq,
-            "m1p": m1p, "he": he, "hr": hr, "hq": hq, "m2p": m2p, "va": va, "sq": sq,
-            "tmax": tmax, "tsqrt": tsqrt, "trec": trec, "sc": sc, "st": st,
-        }
-        for entry in PROGRAM:
-            steps[entry[0]](*entry[1:])
+        ld_x(0, 1)
+        ld_w1(0, 0)
+        ld_x(1, 1)
+        ld_x(2, 1)
+        ld_x(3, 1)
+        ld_w1(1, 0)
+        ld_b()
+        ld_w1(0, 1)
+        ld_w1(1, 1)
+        ld_x(4, 2)
+        ld_x(6, 2)
+        ld_w2(0)
+        ld_w2(1)
+
+        xt(0)
+        xe(0, "S")
+        w1r(0, 0, 0, "V")
+        w1r(0, 0, 1, "V")
+        xt(1)
+        xe(1, "S")
+        xt(2)
+        xt(3)
+        w1q(0, 0)
+        xe(2, "V")
+        xe(3, "S")
+        w1r(1, 0, 0, "V")
+        w1r(1, 0, 1, "S")
+        xq(0, 0)
+        xq(1, 0)
+        for t in range(4):
+            m1(0, t, 0, 0)
+        w1q(1, 0)
+        w1r(0, 1, 0, "S")
+        w1r(0, 1, 1, "S")
+        for t in range(4):
+            m1(0, t, 0, 1)
+        w1r(1, 1, 0, "V")
+        w1r(1, 1, 1, "V")
+        w1q(0, 1)
+        for r in range(4, 8):
+            xt(r)
+        for t in range(4):
+            he(0, t, 0, "S")
+        w1q(1, 1)
+        xe(4, "V")
+        xe(5, "V")
+        for t in range(4):
+            m1(1, t, 0, 0)
+        for t in range(4):
+            m1(1, t, 0, 1)
+        xe(6, "S")
+
+        hr(0, 0, 0, "V")
+        hr(0, 0, 1, "V")
+        xe(7, "S")
+        b2_spread()
+        w2s(0, 0)
+        w2s(0, 1)
+        xq(0, 1)
+        xq(1, 1)
+        for t in range(3):
+            he(1, t, 0, "S")
+        he(1, 3, 0, "V")
+        hq(0, 0)
+        w2e(0, 0, "S")
+        w2e(0, 1, "S")
+        for t in range(4):
+            m1(0, t, 1, 0)
+            m1(0, t, 1, 1)
+        hr(1, 0, 0, "V")
+        hr(1, 0, 1, "V")
+        he(0, 0, 1, "S")
+        b2_copy("S")
+        w2q(0)
+        he(0, 1, 1, "S")
+        w2s(1, 0)
+        w2s(1, 1)
+        he(0, 2, 1, "S")
+        he(0, 3, 1, "V")
+        hq(1, 0)
+        for t in range(4):
+            m1(1, t, 1, 0)
+            m1(1, t, 1, 1)
+        w2e(1, 0, "S")
+        w2e(1, 1, "V")
+        hr(0, 1, 0, "V")
+        he(1, 0, 1, "S")
+        he(1, 1, 1, "S")
+        hr(0, 1, 1, "V")
+        w2q(1)
+        he(1, 2, 1, "S")
+        he(1, 3, 1, "S")
+        for r in range(4):
+            m2(r, 0)
+            m2(r, 1)
+        hq(0, 1)
+        va(0)
+        hr(1, 1, 0, "V")
+        hr(1, 1, 1, "S")
+        va(1)
+        va(2)
+        for r in range(4, 8):
+            m2(r, 0)
+        hq(1, 1)
+        va(3)
+        sq(0)
+        sq(1)
+        norm(0, 2)
+        sq(2)
+        for r in range(4, 8):
+            m2(r, 1)
+        sc(0, "V")
+        sc(1, "V")
+        st(0, 2)
+        sq(3)
+        norm(2, 2)
+        va(4)
+        va(5)
+        sc(2, "V")
+        sc(3, "V")
+        st(2, 2)
+        sq(4)
+        va(6)
+        sq(5)
+        norm(4, 2)
+        va(7)
+        sc(4, "V")
+        sq(6)
+        norm(6, 1)
+        sc(5, "V")
+        st(4, 2)
+        sq(7)
+        norm(7, 1)
+        sc(6, "V")
+        st(6, 1)
+        sc(7, "V")
+        st(7, 1)

@@ -51,6 +51,8 @@ def tile_geometricmanifoldnetwork_pa_kernel(tc, x, W1, b1, W2, b2, out):
         make_identity(nc, ident_f[:])
         ident_b = get("ident_b", [P, P], BF16)
         nc.vector.tensor_copy(out=ident_b[:], in_=ident_f[:])
+        zeros = get("zeros", [P, 512], BF16)
+        nc.gpsimd.memset(zeros[:], 0.0)
         b1t = get("b1t", [P, 2, 4], BF16)
         b2bc = get("b2bc", [P, M], F32)
 
@@ -101,6 +103,11 @@ def tile_geometricmanifoldnetwork_pa_kernel(tc, x, W1, b1, W2, b2, out):
 
         def b2_copy(e):
             copy_on(e, b2bc[:], tiles["pb2"][:])
+
+        def wake(n):
+            for i in range(n):
+                wk = bank("wk", [P, 512], F32)
+                nc.tensor.matmul(out=wk[:], lhsT=ones_b[:], rhs=zeros[:], start=True, stop=True)
 
         def xt(r):
             pt = bank("pt_%d" % r, [P, 2, 2, P], F32)
@@ -249,6 +256,7 @@ def tile_geometricmanifoldnetwork_pa_kernel(tc, x, W1, b1, W2, b2, out):
         ld_w2(0)
         ld_w2(1)
 
+        wake(4)
         xt(0)
         xe(0, "S")
         w1r(0, 0, 0, "V")
@@ -280,51 +288,45 @@ def tile_geometricmanifoldnetwork_pa_kernel(tc, x, W1, b1, W2, b2, out):
             he(0, t, 0, "S")
         w1q(1, 1)
         xe(4, "V")
-        xe(5, "V")
         for t in range(4):
             m1(1, t, 0, 0)
         for t in range(4):
             m1(1, t, 0, 1)
+        xe(5, "S")
         xe(6, "S")
-
         hr(0, 0, 0, "V")
         hr(0, 0, 1, "V")
         xe(7, "S")
         b2_spread()
-        w2s(0, 0)
-        w2s(0, 1)
+        w2r(0, 0, "V")
         xq(0, 1)
         xq(1, 1)
-        for t in range(3):
+        for t in range(4):
             he(1, t, 0, "S")
-        he(1, 3, 0, "V")
         hq(0, 0)
-        w2e(0, 0, "S")
-        w2e(0, 1, "S")
+        w2r(0, 1, "V")
         for t in range(4):
             m1(0, t, 1, 0)
             m1(0, t, 1, 1)
+        w2q(0)
         hr(1, 0, 0, "V")
         hr(1, 0, 1, "V")
+        w2r(1, 0, "V")
         he(0, 0, 1, "S")
-        b2_copy("S")
-        w2q(0)
         he(0, 1, 1, "S")
-        w2s(1, 0)
-        w2s(1, 1)
         he(0, 2, 1, "S")
-        he(0, 3, 1, "V")
+        he(0, 3, 1, "S")
         hq(1, 0)
         for t in range(4):
             m1(1, t, 1, 0)
             m1(1, t, 1, 1)
-        w2e(1, 0, "S")
-        w2e(1, 1, "V")
+        w2r(1, 1, "V")
         hr(0, 1, 0, "V")
+        w2q(1)
+        hr(0, 1, 1, "V")
         he(1, 0, 1, "S")
         he(1, 1, 1, "S")
-        hr(0, 1, 1, "V")
-        w2q(1)
+        b2_copy("S")
         he(1, 2, 1, "S")
         he(1, 3, 1, "S")
         for r in range(4):
@@ -347,7 +349,7 @@ def tile_geometricmanifoldnetwork_pa_kernel(tc, x, W1, b1, W2, b2, out):
         for r in range(4, 8):
             m2(r, 1)
         sc(0, "V")
-        sc(1, "V")
+        sc(1, "S")
         st(0, 2)
         sq(3)
         norm(2, 2)

@@ -40,8 +40,6 @@ def tile_geometricmanifoldnetwork_pa_kernel(tc, x, W1, b1, W2, b2, out):
             tiles[key] = ps.tile(shape, dtype, name="bank", tag="bank")
             return tiles[key]
 
-        b2row = get("b2row", [P, M], BF16)
-        nc.vector.memset(b2row[:], 0.0)
         ones_b = get("ones_b", [P, P], BF16)
         nc.vector.memset(ones_b[:], 1.0)
         warm = get("warm", [P, 2], F32)
@@ -49,12 +47,10 @@ def tile_geometricmanifoldnetwork_pa_kernel(tc, x, W1, b1, W2, b2, out):
         nc.scalar.activation(out=warm[:, 1:2], in_=warm[:, 0:1], func=ACT.Abs_reciprocal_sqrt)
         ident_f = get("ident_f", [P, P], F32)
         make_identity(nc, ident_f[:])
-        ident_b = get("ident_b", [P, P], BF16)
-        nc.vector.tensor_copy(out=ident_b[:], in_=ident_f[:])
         zeros = get("zeros", [P, 512], BF16)
         nc.gpsimd.memset(zeros[:], 0.0)
         b1t = get("b1t", [P, 2, 4], BF16)
-        b2bc = get("b2bc", [P, M], F32)
+        b2bc = get("b2bc", [P, M], BF16)
 
         def copy_on(e, dst, src):
             if e == "V":
@@ -67,14 +63,13 @@ def tile_geometricmanifoldnetwork_pa_kernel(tc, x, W1, b1, W2, b2, out):
             scales = get("s_" + name, [P, 512], U8)
             nc.vector.quantize_mx(out=codes[:].bitcast(FP8X4), scales=scales[:], in_=src)
 
-        def mx_pass(acc, lhs_name, r, rhs_name, start, stop):
-            cols = slice(P * r, P * r + P)
+        def mx_pass(acc, lhs_name, lcols, rhs_name, rcols, start, stop):
             nc.tensor.matmul_mx(
-                out=acc[:],
-                lhsT=tiles["c_" + lhs_name][:, cols].bitcast(FP8X4),
-                lhsT_scale=tiles["s_" + lhs_name][:, cols],
-                rhs=tiles["c_" + rhs_name][:].bitcast(FP8X4),
-                rhs_scale=tiles["s_" + rhs_name][:],
+                out=acc,
+                lhsT=tiles["c_" + lhs_name][:, lcols].bitcast(FP8X4),
+                lhsT_scale=tiles["s_" + lhs_name][:, lcols],
+                rhs=tiles["c_" + rhs_name][:, rcols].bitcast(FP8X4),
+                rhs_scale=tiles["s_" + rhs_name][:, rcols],
                 start=start,
                 stop=stop,
             )
@@ -95,14 +90,9 @@ def tile_geometricmanifoldnetwork_pa_kernel(tc, x, W1, b1, W2, b2, out):
 
         def ld_b():
             nc.sync.dma_start(out=b1t[:], in_=b1.rearrange("(g p t) -> p g t", g=2, t=4))
-            nc.sync.dma_start(out=b2row[0:1, :], in_=b2.rearrange("(o m) -> o m", o=1))
 
-        def b2_spread():
-            pb2 = bank("pb2", [P, M], F32)
-            nc.tensor.matmul(out=pb2[:], lhsT=ones_b[:], rhs=b2row[:], start=True, stop=True)
-
-        def b2_copy(e):
-            copy_on(e, b2bc[:], tiles["pb2"][:])
+        def ld_b2():
+            nc.sync.dma_start(out=b2bc[:], in_=b2.partition_broadcast(P))
 
         def wake(n):
             for i in range(n):
@@ -118,13 +108,13 @@ def tile_geometricmanifoldnetwork_pa_kernel(tc, x, W1, b1, W2, b2, out):
                     nc.tensor.transpose(out=pt[:, g, u, :], in_=words[:, c0 + u : c0 + 256 : 2], identity=ident_f[:])
 
         def xe(r, e):
-            bh, i = divmod(r, 4)
-            gx = get("g_x_%d" % bh, [P, 4096], BF16)
-            dst = gx[:].bitcast(F32).rearrange("p (g i b u) -> p i g b u", g=2, i=4, u=2)[:, i, :, :, :]
+            q, i = divmod(r, 2)
+            gx = get("g_x_%d" % q, [P, 2048], BF16)
+            dst = gx[:].bitcast(F32).rearrange("p (g i b u) -> p i g b u", g=2, i=2, u=2)[:, i, :, :, :]
             copy_on(e, dst, tiles["pt_%d" % r][:].rearrange("p g u b -> p g b u"))
 
-        def xq(g, bh):
-            quantise("x_%d%d" % (g, bh), tiles["g_x_%d" % bh][:, 2048 * g : 2048 * g + 2048])
+        def xq(q):
+            quantise("x_%d" % q, tiles["g_x_%d" % q][:])
 
         def w1_tile(g, fh):
             return get("g_w1_%d%d" % (g, fh), [P, 2048], BF16)
@@ -136,17 +126,6 @@ def tile_geometricmanifoldnetwork_pa_kernel(tc, x, W1, b1, W2, b2, out):
                 w1_tile(g, fh)[:].rearrange("p (t m j) -> p m j t", t=4, j=4)[:, ms, :, :],
                 tiles["raw1_%d%d" % (g, fh)][:].rearrange("p j (m t) -> p m j t", t=4)[:, ms, :, :],
             )
-
-        def w1s(g, fh, h):
-            pw = bank("pw1_%d%d%d" % (g, fh, h), [P, 2, 512], BF16)
-            src = tiles["raw1_%d%d" % (g, fh)][:].rearrange("p j (m t) -> p t m j", t=4)
-            for i in range(2):
-                nc.tensor.matmul(out=pw[:, i, :], lhsT=ident_b[:], rhs=src[:, 2 * h + i, :, :], start=True, stop=True)
-
-        def w1e(g, fh, h, e):
-            pw = tiles["pw1_%d%d%d" % (g, fh, h)]
-            dst = w1_tile(g, fh)[:, 1024 * h : 1024 * h + 1024].bitcast(F32)
-            copy_on(e, dst, pw[:].rearrange("p i c -> p (i c)").bitcast(F32))
 
         def w1q(g, fh):
             quantise("w1_%d%d" % (g, fh), w1_tile(g, fh)[:])
@@ -165,50 +144,60 @@ def tile_geometricmanifoldnetwork_pa_kernel(tc, x, W1, b1, W2, b2, out):
         def w2r(g, h, e):
             regroup(e, w2_tile(g), tiles["raw2_%d" % g], h)
 
-        def w2s(g, h):
-            pw = bank("pw2_%d%d" % (g, h), [P, 2, 512], BF16)
-            src = tiles["raw2_%d" % g][:].rearrange("p j c -> p c j")
-            for i in range(2):
-                c0 = 256 * h + 128 * i
-                nc.tensor.matmul(out=pw[:, i, :], lhsT=ident_b[:], rhs=src[:, c0 : c0 + 128, :], start=True, stop=True)
-
-        def w2e(g, h, e):
-            dst = w2_tile(g)[:, 1024 * h : 1024 * h + 1024].bitcast(F32)
-            copy_on(e, dst, tiles["pw2_%d%d" % (g, h)][:].rearrange("p i c -> p (i c)").bitcast(F32))
-
         def w2q(g):
             quantise("w2_%d" % g, w2_tile(g)[:])
 
-        def m1(fh, t, bh, g):
-            key = "ph_%d%d%d" % (fh, t, bh)
-            if g == 0:
-                bank(key, [P, 512], F32)
-            mx_pass(tiles[key], "w1_%d%d" % (g, fh), t, "x_%d%d" % (g, bh), g == 0, g == 1)
+        def m1(fh, t2, q):
+            ph = bank("ph_%d%d%d" % (fh, t2, q), [P, 2, 256], F32)
+            for i in range(2):
+                t = 2 * t2 + i
+                for g in range(2):
+                    mx_pass(
+                        ph[:, i, :], "w1_%d%d" % (g, fh), slice(P * t, P * t + P),
+                        "x_%d" % q, slice(256 * g, 256 * g + 256), g == 0, g == 1,
+                    )
 
-        def he(fh, t, bh, e):
-            ht = get("ht_%d%d" % (fh, bh), [P, 4, 512], BF16)
-            ph = tiles["ph_%d%d%d" % (fh, t, bh)]
-            bias = b1t[:, fh, t : t + 1]
-            if e == "V":
-                nc.vector.tensor_scalar(
-                    out=ht[:, t, :], in0=ph[:], scalar1=bias, scalar2=0.0, op0=ALU.add, op1=ALU.max
-                )
-            else:
-                nc.scalar.activation(out=ht[:, t, :], in_=ph[:], func=ACT.Relu, bias=bias, scale=1.0)
+        def he(fh, t2, q, e):
+            ht = get("ht_%d%d" % (fh, q), [P, 4, 256], BF16)
+            ph = tiles["ph_%d%d%d" % (fh, t2, q)]
+            for i in range(2):
+                t = 2 * t2 + i
+                bias = b1t[:, fh, t : t + 1]
+                if e == "V":
+                    nc.vector.tensor_scalar(
+                        out=ht[:, t, :], in0=ph[:, i, :], scalar1=bias, scalar2=0.0, op0=ALU.add, op1=ALU.max
+                    )
+                else:
+                    nc.scalar.activation(out=ht[:, t, :], in_=ph[:, i, :], func=ACT.Relu, bias=bias, scale=1.0)
 
-        def hr(fh, bh, h, e):
-            regroup(e, get("g_h_%d%d" % (fh, bh), [P, 2048], BF16), tiles["ht_%d%d" % (fh, bh)], h)
+        def hr(fh, q, e):
+            gh = get("g_h_%d" % q, [P, 2048], BF16)
+            copy_on(
+                e,
+                gh[:, 1024 * fh : 1024 * fh + 1024].rearrange("p (c i t) -> p c t i", i=4, t=4),
+                tiles["ht_%d%d" % (fh, q)][:].rearrange("p t (c i) -> p c t i", i=4),
+            )
 
-        def hq(fh, bh):
-            quantise("h_%d%d" % (fh, bh), tiles["g_h_%d%d" % (fh, bh)][:])
+        def hq(q, f0, n):
+            codes = get("c_h_%d" % q, [P, 512], U32)
+            scales = get("s_h_%d" % q, [P, 512], U8)
+            c = slice(256 * f0, 256 * (f0 + n))
+            nc.vector.quantize_mx(
+                out=codes[:, c].bitcast(FP8X4), scales=scales[:, c],
+                in_=tiles["g_h_%d" % q][:, 1024 * f0 : 1024 * (f0 + n)],
+            )
 
-        def m2(r, g):
+        def m2p(r, g):
+            q, i = divmod(r, 2)
             key = "pv_%d" % r
             if g == 0:
                 bank(key, [P, M], F32)
-            bh, i = divmod(r, 4)
-            mx_pass(tiles[key], "h_%d%d" % (g, bh), i, "w2_%d" % g, g == 0, g == 1)
+            c0 = 256 * g + P * i
+            mx_pass(tiles[key][:], "h_%d" % q, slice(c0, c0 + P), "w2_%d" % g, slice(0, M), g == 0, g == 1)
 
+        def m2(r):
+            m2p(r, 0)
+            m2p(r, 1)
         def va(r):
             v = get("v_%d" % r, [P, M], F32)
             nc.vector.tensor_tensor(out=v[:], in0=tiles["pv_%d" % r][:], in1=b2bc[:], op=ALU.add)
@@ -219,14 +208,13 @@ def tile_geometricmanifoldnetwork_pa_kernel(tc, x, W1, b1, W2, b2, out):
             i = r % 2
             nc.scalar.activation(out=junk[:], in_=tiles["v_%d" % r][:], func=ACT.Square, accum_out=ss[:, i : i + 1])
 
-        def norm(r, n):
-            u, i = divmod(r, 2)
-            ss = tiles["ss_%d" % u]
+        def clamp(u):
             over = get("over_%d" % u, [P, 2], F32)
+            nc.scalar.activation(out=over[:], in_=tiles["ss_%d" % u][:], func=ACT.Relu, bias=-EPS * EPS)
+
+        def rsq(u):
             rinv = get("rinv_%d" % u, [P, 2], F32)
-            c = slice(i, i + n)
-            nc.scalar.activation(out=over[:, c], in_=ss[:, c], func=ACT.Relu, bias=-EPS * EPS)
-            nc.scalar.activation(out=rinv[:, c], in_=over[:, c], func=ACT.Abs_reciprocal_sqrt, bias=EPS * EPS)
+            nc.scalar.activation(out=rinv[:], in_=tiles["over_%d" % u][:], func=ACT.Abs_reciprocal_sqrt, bias=EPS * EPS)
 
         def sc(r, e):
             o = get("o_%d" % (r // 2), [P, 2, M], F32)
@@ -235,8 +223,10 @@ def tile_geometricmanifoldnetwork_pa_kernel(tc, x, W1, b1, W2, b2, out):
             v = tiles["v_%d" % r]
             if e == "V":
                 nc.vector.tensor_scalar_mul(out=o[:, i, :], in0=v[:], scalar1=rinv)
-            else:
+            elif e == "S":
                 nc.scalar.activation(out=o[:, i, :], in_=v[:], func=ACT.Copy, scale=rinv)
+            else:
+                nc.gpsimd.tensor_scalar(out=o[:, i, :], in0=v[:], scalar1=rinv, scalar2=0.0, op0=ALU.mult, op1=ALU.add)
 
         def st(r, n):
             i = r % 2
@@ -245,16 +235,16 @@ def tile_geometricmanifoldnetwork_pa_kernel(tc, x, W1, b1, W2, b2, out):
         ld_x(0, 1)
         ld_w1(0, 0)
         ld_x(1, 1)
-        ld_x(2, 1)
-        ld_x(3, 1)
         ld_w1(1, 0)
-        ld_b()
         ld_w1(0, 1)
         ld_w1(1, 1)
+        ld_b()
+        ld_x(2, 2)
         ld_x(4, 2)
-        ld_x(6, 2)
         ld_w2(0)
         ld_w2(1)
+        ld_x(6, 2)
+        ld_b2()
 
         wake(4)
         xt(0)
@@ -263,113 +253,127 @@ def tile_geometricmanifoldnetwork_pa_kernel(tc, x, W1, b1, W2, b2, out):
         w1r(0, 0, 1, "V")
         xt(1)
         xe(1, "S")
-        xt(2)
-        xt(3)
+        wake(4)
         w1q(0, 0)
-        xe(2, "V")
-        xe(3, "S")
         w1r(1, 0, 0, "V")
         w1r(1, 0, 1, "S")
-        xq(0, 0)
-        xq(1, 0)
-        for t in range(4):
-            m1(0, t, 0, 0)
+        xq(0)
         w1q(1, 0)
         w1r(0, 1, 0, "S")
-        w1r(0, 1, 1, "S")
-        for t in range(4):
-            m1(0, t, 0, 1)
+        w1r(0, 1, 1, "V")
+        m1(0, 0, 0)
+        m1(0, 1, 0)
         w1r(1, 1, 0, "V")
         w1r(1, 1, 1, "V")
+        he(0, 0, 0, "S")
+        he(0, 1, 0, "S")
         w1q(0, 1)
-        for r in range(4, 8):
-            xt(r)
-        for t in range(4):
-            he(0, t, 0, "S")
         w1q(1, 1)
-        xe(4, "V")
-        for t in range(4):
-            m1(1, t, 0, 0)
-        for t in range(4):
-            m1(1, t, 0, 1)
-        xe(5, "S")
-        xe(6, "S")
-        hr(0, 0, 0, "V")
-        hr(0, 0, 1, "V")
-        xe(7, "S")
-        b2_spread()
+        xt(2)
+        xt(3)
+        xe(2, "S")
+        xe(3, "S")
+        m1(1, 0, 0)
+        m1(1, 1, 0)
+        xt(4)
+        xt(5)
+        hr(0, 0, "V")
+        xq(1)
+        he(1, 0, 0, "S")
+        he(1, 1, 0, "S")
+        xe(4, "S")
         w2r(0, 0, "V")
-        xq(0, 1)
-        xq(1, 1)
-        for t in range(4):
-            he(1, t, 0, "S")
-        hq(0, 0)
-        w2r(0, 1, "V")
-        for t in range(4):
-            m1(0, t, 1, 0)
-            m1(0, t, 1, 1)
-        w2q(0)
-        hr(1, 0, 0, "V")
-        hr(1, 0, 1, "V")
-        w2r(1, 0, "V")
+        xe(5, "S")
+        m1(0, 0, 1)
+        m1(0, 1, 1)
+        m1(1, 0, 1)
+        m1(1, 1, 1)
+        hr(1, 0, "V")
+        hq(0, 0, 2)
+        xq(2)
         he(0, 0, 1, "S")
         he(0, 1, 1, "S")
-        he(0, 2, 1, "S")
-        he(0, 3, 1, "S")
-        hq(1, 0)
-        for t in range(4):
-            m1(1, t, 1, 0)
-            m1(1, t, 1, 1)
-        w2r(1, 1, "V")
-        hr(0, 1, 0, "V")
-        w2q(1)
-        hr(0, 1, 1, "V")
+        xt(6)
+        xt(7)
         he(1, 0, 1, "S")
         he(1, 1, 1, "S")
-        b2_copy("S")
-        he(1, 2, 1, "S")
-        he(1, 3, 1, "S")
-        for r in range(4):
-            m2(r, 0)
-            m2(r, 1)
-        hq(0, 1)
+        w2r(0, 1, "V")
+        w2q(0)
+        m1(0, 0, 2)
+        m1(0, 1, 2)
+        m1(1, 0, 2)
+        m1(1, 1, 2)
+        w2r(1, 0, "S")
+        xe(6, "S")
+        xe(7, "S")
+        hr(0, 1, "V")
+        hr(1, 1, "V")
+        w2r(1, 1, "V")
+        hq(1, 0, 2)
+        w2q(1)
+        he(0, 0, 2, "S")
+        he(0, 1, 2, "S")
+        xq(3)
+        he(1, 0, 2, "S")
+        he(1, 1, 2, "S")
+        m2(0)
+        m2(1)
+        m1(0, 0, 3)
+        m1(0, 1, 3)
+        m1(1, 0, 3)
+        m1(1, 1, 3)
+        m2(2)
+        m2(3)
+        hr(0, 2, "V")
+        he(0, 0, 3, "S")
+        he(0, 1, 3, "S")
         va(0)
-        hr(1, 1, 0, "V")
-        hr(1, 1, 1, "S")
+        hr(1, 2, "V")
         va(1)
-        va(2)
-        for r in range(4, 8):
-            m2(r, 0)
-        hq(1, 1)
-        va(3)
+        he(1, 0, 3, "S")
+        he(1, 1, 3, "S")
+        hq(2, 0, 2)
         sq(0)
+        va(2)
+        hr(0, 3, "V")
         sq(1)
-        norm(0, 2)
+        clamp(0)
+        va(3)
+        hq(3, 0, 1)
+        hr(1, 3, "V")
+        m2(4)
+        m2(5)
+        m2p(6, 0)
+        m2p(7, 0)
         sq(2)
-        for r in range(4, 8):
-            m2(r, 1)
-        sc(0, "V")
+        rsq(0)
+        sq(3)
+        sc(0, "S")
+        clamp(1)
         sc(1, "S")
         st(0, 2)
-        sq(3)
-        norm(2, 2)
+        rsq(1)
         va(4)
-        va(5)
-        sc(2, "V")
-        sc(3, "V")
+        hq(3, 1, 1)
+        sc(2, "G")
+        sc(3, "G")
         st(2, 2)
+        m2p(6, 1)
+        m2p(7, 1)
         sq(4)
+        va(5)
         va(6)
-        sq(5)
-        norm(4, 2)
         va(7)
-        sc(4, "V")
+        sq(5)
+        clamp(2)
         sq(6)
-        norm(6, 1)
+        rsq(2)
+        sq(7)
+        clamp(3)
+        rsq(3)
+        sc(4, "V")
         sc(5, "V")
         st(4, 2)
-        sq(7)
-        norm(7, 1)
         sc(6, "V")
         st(6, 1)
         sc(7, "V")

@@ -119,12 +119,11 @@ def tile_geometricmanifoldnetwork_pa_kernel(tc, x, W1, b1, W2, b2, out):
         def w1_tile(g, fh):
             return get("g_w1_%d%d" % (g, fh), [P, 2048], BF16)
 
-        def w1r(g, fh, h, e):
-            ms = slice(64 * h, 64 * h + 64)
+        def w1r(g, fh, t, e):
             copy_on(
                 e,
-                w1_tile(g, fh)[:].rearrange("p (t m j) -> p m j t", t=4, j=4)[:, ms, :, :],
-                tiles["raw1_%d%d" % (g, fh)][:].rearrange("p j (m t) -> p m j t", t=4)[:, ms, :, :],
+                w1_tile(g, fh)[:, 512 * t : 512 * t + 512].rearrange("p (c i j) -> p c j i", i=4, j=4),
+                tiles["raw1_%d%d" % (g, fh)][:].rearrange("p j (c i t) -> p t c j i", i=4, t=4)[:, t, :, :, :],
             )
 
         def w1q(g, fh):
@@ -249,28 +248,32 @@ def tile_geometricmanifoldnetwork_pa_kernel(tc, x, W1, b1, W2, b2, out):
         wake(4)
         xt(0)
         xe(0, "S")
-        w1r(0, 0, 0, "V")
-        w1r(0, 0, 1, "V")
+        for t in range(4):
+            w1r(0, 0, t, "V")
         xt(1)
         xe(1, "S")
         wake(4)
         w1q(0, 0)
-        w1r(1, 0, 0, "V")
-        w1r(1, 0, 1, "S")
+        for t in range(2):
+            w1r(1, 0, t, "V")
+            w1r(1, 0, t + 2, "S")
         xq(0)
         w1q(1, 0)
-        w1r(0, 1, 0, "S")
-        w1r(0, 1, 1, "V")
+        for t in range(2):
+            w1r(0, 1, t, "S")
+            w1r(0, 1, t + 2, "V")
         m1(0, 0, 0)
         m1(0, 1, 0)
-        w1r(1, 1, 0, "V")
-        w1r(1, 1, 1, "V")
+        for t in range(4):
+            w1r(1, 1, t, "V")
         he(0, 0, 0, "S")
         he(0, 1, 0, "S")
         w1q(0, 1)
         w1q(1, 1)
+        wake(2)
         xt(2)
         xt(3)
+        wake(1)
         xe(2, "S")
         xe(3, "S")
         m1(1, 0, 0)
@@ -289,6 +292,7 @@ def tile_geometricmanifoldnetwork_pa_kernel(tc, x, W1, b1, W2, b2, out):
         m1(1, 0, 1)
         m1(1, 1, 1)
         hr(1, 0, "V")
+        w2r(0, 1, "V")
         hq(0, 0, 2)
         xq(2)
         he(0, 0, 1, "S")
@@ -297,7 +301,6 @@ def tile_geometricmanifoldnetwork_pa_kernel(tc, x, W1, b1, W2, b2, out):
         xt(7)
         he(1, 0, 1, "S")
         he(1, 1, 1, "S")
-        w2r(0, 1, "V")
         w2q(0)
         m1(0, 0, 2)
         m1(0, 1, 2)
@@ -366,8 +369,8 @@ def tile_geometricmanifoldnetwork_pa_kernel(tc, x, W1, b1, W2, b2, out):
         va(7)
         sq(5)
         clamp(2)
-        sq(6)
         rsq(2)
+        sq(6)
         sq(7)
         clamp(3)
         rsq(3)

@@ -238,7 +238,8 @@ def tile_geometricmanifoldnetwork_pa_kernel(tc, x, W1, b1, W2, b2, out):
         ld_w1(0, 1)
         ld_w1(1, 1)
         ld_b()
-        ld_x(2, 2)
+        ld_x(2, 1)
+        ld_x(3, 1)
         ld_x(4, 2)
         ld_w2(0)
         ld_w2(1)
@@ -333,13 +334,13 @@ def tile_geometricmanifoldnetwork_pa_kernel(tc, x, W1, b1, W2, b2, out):
         va(0)
         hr(1, 2, "V")
         va(1)
-        he(1, 0, 3, "S")
-        he(1, 1, 3, "S")
-        hq(2, 0, 2)
         sq(0)
-        va(2)
+        he(1, 0, 3, "S")
+        hq(2, 0, 2)
         hr(0, 3, "V")
+        va(2)
         sq(1)
+        he(1, 1, 3, "S")
         clamp(0)
         va(3)
         hq(3, 0, 1)
@@ -351,11 +352,11 @@ def tile_geometricmanifoldnetwork_pa_kernel(tc, x, W1, b1, W2, b2, out):
         sq(2)
         rsq(0)
         sq(3)
-        sc(0, "S")
         clamp(1)
+        sc(0, "S")
+        rsq(1)
         sc(1, "S")
         st(0, 2)
-        rsq(1)
         va(4)
         hq(3, 1, 1)
         sc(2, "G")

@@ -353,9 +353,9 @@ def tile_geometricmanifoldnetwork_pa_kernel(tc, x, W1, b1, W2, b2, out):
         rsq(0)
         sq(3)
         clamp(1)
-        sc(0, "S")
+        sc(0, "G")
         rsq(1)
-        sc(1, "S")
+        sc(1, "G")
         st(0, 2)
         va(4)
         hq(3, 1, 1)

@@ -40,15 +40,11 @@ def tile_geometricmanifoldnetwork_pa_kernel(tc, x, W1, b1, W2, b2, out):
             tiles[key] = ps.tile(shape, dtype, name="bank", tag="bank")
             return tiles[key]
 
-        ones_b = get("ones_b", [P, P], BF16)
-        nc.vector.memset(ones_b[:], 1.0)
         warm = get("warm", [P, 2], F32)
         nc.vector.memset(warm[:], 1.0)
         nc.scalar.activation(out=warm[:, 1:2], in_=warm[:, 0:1], func=ACT.Abs_reciprocal_sqrt)
         ident_f = get("ident_f", [P, P], F32)
         make_identity(nc, ident_f[:])
-        zeros = get("zeros", [P, 512], BF16)
-        nc.gpsimd.memset(zeros[:], 0.0)
         b1t = get("b1t", [P, 2, 4], BF16)
         b2bc = get("b2bc", [P, M], BF16)
 
@@ -93,11 +89,6 @@ def tile_geometricmanifoldnetwork_pa_kernel(tc, x, W1, b1, W2, b2, out):
 
         def ld_b2():
             nc.sync.dma_start(out=b2bc[:], in_=b2.partition_broadcast(P))
-
-        def wake(n):
-            for i in range(n):
-                wk = bank("wk", [P, 512], F32)
-                nc.tensor.matmul(out=wk[:], lhsT=ones_b[:], rhs=zeros[:], start=True, stop=True)
 
         def xt(r):
             pt = bank("pt_%d" % r, [P, 2, 2, P], F32)
@@ -246,14 +237,12 @@ def tile_geometricmanifoldnetwork_pa_kernel(tc, x, W1, b1, W2, b2, out):
         ld_x(6, 2)
         ld_b2()
 
-        wake(4)
         xt(0)
         xe(0, "S")
         for t in range(4):
             w1r(0, 0, t, "V")
         xt(1)
         xe(1, "S")
-        wake(4)
         w1q(0, 0)
         for t in range(2):
             w1r(1, 0, t, "V")
@@ -271,10 +260,8 @@ def tile_geometricmanifoldnetwork_pa_kernel(tc, x, W1, b1, W2, b2, out):
         he(0, 1, 0, "S")
         w1q(0, 1)
         w1q(1, 1)
-        wake(2)
         xt(2)
         xt(3)
-        wake(1)
         xe(2, "S")
         xe(3, "S")
         m1(1, 0, 0)

from contextlib import ExitStack

import concourse.mybir as mybir
from concourse.masks import make_identity

F32 = mybir.dt.float32
BF16 = mybir.dt.bfloat16
U32 = mybir.dt.uint32
U8 = mybir.dt.uint8
FP8X4 = mybir.dt.float8_e4m3fn_x4
ACT = mybir.ActivationFunctionType
ALU = mybir.AluOpType

P = 128
B, IN, F, M = 1024, 1024, 1024, 512
FLOPS = 2 * B * IN * F + 2 * B * F * M
EPS = 1e-12


def tile_geometricmanifoldnetwork_pa_kernel(tc, x, W1, b1, W2, b2, out):
    nc = tc.nc
    with ExitStack() as ctx:
        sb = ctx.enter_context(tc.tile_pool(name="sb", bufs=1))
        ps = ctx.enter_context(tc.psum_pool(name="ps", bufs=8))
        ctx.enter_context(tc.manual_schedule())

        x_v = x.rearrange("(p r) k -> p r k", r=8)
        out_v = out.rearrange("(p r) m -> p r m", r=8)
        w1_v = W1.rearrange("(g p j) f -> g p j f", g=2, j=4)
        w2_v = W2.rearrange("(g p j) m -> g p j m", g=2, j=4)

        tiles = {}

        def get(key, shape, dtype):
            if key not in tiles:
                tiles[key] = sb.tile(shape, dtype, name=key, align_bytes=64)
            return tiles[key]

        def bank(key, shape, dtype):
            tiles[key] = ps.tile(shape, dtype, name="bank", tag="bank")
            return tiles[key]

        warm = get("warm", [P, 2], F32)
        nc.vector.memset(warm[:], 1.0)
        nc.scalar.activation(out=warm[:, 1:2], in_=warm[:, 0:1], func=ACT.Abs_reciprocal_sqrt)
        ident_f = get("ident_f", [P, P], F32)
        make_identity(nc, ident_f[:])
        b1t = get("b1t", [P, 2, 4], BF16)
        b2bc = get("b2bc", [P, M], BF16)

        def copy_on(e, dst, src):
            if e == "V":
                nc.vector.tensor_copy(out=dst, in_=src)
            else:
                nc.scalar.copy(out=dst, in_=src)

        def quantise(name, src):
            codes = get("c_" + name, [P, 512], U32)
            scales = get("s_" + name, [P, 512], U8)
            nc.vector.quantize_mx(out=codes[:].bitcast(FP8X4), scales=scales[:], in_=src)

        def mx_pass(acc, lhs_name, lcols, rhs_name, rcols, start, stop):
            nc.tensor.matmul_mx(
                out=acc,
                lhsT=tiles["c_" + lhs_name][:, lcols].bitcast(FP8X4),
                lhsT_scale=tiles["s_" + lhs_name][:, lcols],
                rhs=tiles["c_" + rhs_name][:, rcols].bitcast(FP8X4),
                rhs_scale=tiles["s_" + rhs_name][:, rcols],
                start=start,
                stop=stop,
            )

        def ld_x(r, n):
            xp = get("x_%d" % r, [P, n, IN], BF16)
            for i in range(n):
                tiles["xr_%d" % (r + i)] = xp[:, i, :]
            nc.sync.dma_start(out=xp[:], in_=x_v[:, r : r + n, :])

        def ld_w1(g, fh):
            raw = get("raw1_%d%d" % (g, fh), [P, 4, 512], BF16)
            nc.sync.dma_start(out=raw[:], in_=w1_v[g, :, :, 512 * fh : 512 * fh + 512])

        def ld_w2(g):
            raw = get("raw2_%d" % g, [P, 4, M], BF16)
            nc.sync.dma_start(out=raw[:], in_=w2_v[g])

        def ld_b():
            nc.sync.dma_start(out=b1t[:], in_=b1.rearrange("(g p t) -> p g t", g=2, t=4))

        def ld_b2():
            nc.sync.dma_start(out=b2bc[:], in_=b2.partition_broadcast(P))

        def xt(r):
            pt = bank("pt_%d" % r, [P, 2, 2, P], F32)
            words = tiles["xr_%d" % r].bitcast(F32)
            for g in range(2):
                for u in range(2):
                    c0 = 256 * g
                    nc.tensor.transpose(out=pt[:, g, u, :], in_=words[:, c0 + u : c0 + 256 : 2], identity=ident_f[:])

        def xe(r, e):
            q, i = divmod(r, 2)
            gx = get("g_x_%d" % q, [P, 2048], BF16)
            dst = gx[:].bitcast(F32).rearrange("p (g i b u) -> p i g b u", g=2, i=2, u=2)[:, i, :, :, :]
            copy_on(e, dst, tiles["pt_%d" % r][:].rearrange("p g u b -> p g b u"))

        def xq(q):
            quantise("x_%d" % q, tiles["g_x_%d" % q][:])

        def w1_tile(g, fh):
            return get("g_w1_%d%d" % (g, fh), [P, 2048], BF16)

        def w1r(g, fh, t, e):
            copy_on(
                e,
                w1_tile(g, fh)[:, 512 * t : 512 * t + 512].rearrange("p (c i j) -> p c j i", i=4, j=4),
                tiles["raw1_%d%d" % (g, fh)][:].rearrange("p j (c i t) -> p t c j i", i=4, t=4)[:, t, :, :, :],
            )

        def w1q(g, fh):
            quantise("w1_%d%d" % (g, fh), w1_tile(g, fh)[:])

        def w2_tile(g):
            return get("g_w2_%d" % g, [P, 2048], BF16)

        def regroup(e, dst, src, h):
            c0 = 256 * h
            copy_on(
                e,
                dst[:, 4 * c0 : 4 * c0 + 1024].rearrange("p (c i t) -> p c t i", i=4, t=4),
                src[:, :, c0 : c0 + 256].rearrange("p t (c i) -> p c t i", i=4),
            )

        def w2r(g, h, e):
            regroup(e, w2_tile(g), tiles["raw2_%d" % g], h)

        def w2q(g):
            quantise("w2_%d" % g, w2_tile(g)[:])

        def m1(fh, t2, q):
            ph = bank("ph_%d%d%d" % (fh, t2, q), [P, 2, 256], F32)
            for i in range(2):
                t = 2 * t2 + i
                for g in range(2):
                    mx_pass(
                        ph[:, i, :], "w1_%d%d" % (g, fh), slice(P * t, P * t + P),
                        "x_%d" % q, slice(256 * g, 256 * g + 256), g == 0, g == 1,
                    )

        def he(fh, t2, q, e):
            ht = get("ht_%d%d" % (fh, q), [P, 4, 256], BF16)
            ph = tiles["ph_%d%d%d" % (fh, t2, q)]
            for i in range(2):
                t = 2 * t2 + i
                bias = b1t[:, fh, t : t + 1]
                if e == "V":
                    nc.vector.tensor_scalar(
                        out=ht[:, t, :], in0=ph[:, i, :], scalar1=bias, scalar2=0.0, op0=ALU.add, op1=ALU.max
                    )
                else:
                    nc.scalar.activation(out=ht[:, t, :], in_=ph[:, i, :], func=ACT.Relu, bias=bias, scale=1.0)

        def hr(fh, q, e):
            gh = get("g_h_%d" % q, [P, 2048], BF16)
            copy_on(
                e,
                gh[:, 1024 * fh : 1024 * fh + 1024].rearrange("p (c i t) -> p c t i", i=4, t=4),
                tiles["ht_%d%d" % (fh, q)][:].rearrange("p t (c i) -> p c t i", i=4),
            )

        def hq(q, f0, n):
            codes = get("c_h_%d" % q, [P, 512], U32)
            scales = get("s_h_%d" % q, [P, 512], U8)
            c = slice(256 * f0, 256 * (f0 + n))
            nc.vector.quantize_mx(
                out=codes[:, c].bitcast(FP8X4), scales=scales[:, c],
                in_=tiles["g_h_%d" % q][:, 1024 * f0 : 1024 * (f0 + n)],
            )

        def m2p(r, g):
            q, i = divmod(r, 2)
            key = "pv_%d" % r
            if g == 0:
                bank(key, [P, M], F32)
            c0 = 256 * g + P * i
            mx_pass(tiles[key][:], "h_%d" % q, slice(c0, c0 + P), "w2_%d" % g, slice(0, M), g == 0, g == 1)

        def m2(r):
            m2p(r, 0)
            m2p(r, 1)
        def va(r):
            v = get("v_%d" % r, [P, M], F32)
            nc.vector.tensor_tensor(out=v[:], in0=tiles["pv_%d" % r][:], in1=b2bc[:], op=ALU.add)

        def sq(r):
            ss = get("ss_%d" % (r // 2), [P, 2], F32)
            junk = get("junk_%d" % (r % 2), [P, M], F32)
            i = r % 2
            nc.scalar.activation(out=junk[:], in_=tiles["v_%d" % r][:], func=ACT.Square, accum_out=ss[:, i : i + 1])

        def clamp(u):
            over = get("over_%d" % u, [P, 2], F32)
            nc.scalar.activation(out=over[:], in_=tiles["ss_%d" % u][:], func=ACT.Relu, bias=-EPS * EPS)

        def rsq(u):
            rinv = get("rinv_%d" % u, [P, 2], F32)
            nc.scalar.activation(out=rinv[:], in_=tiles["over_%d" % u][:], func=ACT.Abs_reciprocal_sqrt, bias=EPS * EPS)

        def sc(r, e):
            o = get("o_%d" % (r // 2), [P, 2, M], F32)
            i = r % 2
            rinv = tiles["rinv_%d" % (r // 2)][:, i : i + 1]
            v = tiles["v_%d" % r]
            if e == "V":
                nc.vector.tensor_scalar_mul(out=o[:, i, :], in0=v[:], scalar1=rinv)
            elif e == "S":
                nc.scalar.activation(out=o[:, i, :], in_=v[:], func=ACT.Copy, scale=rinv)
            else:
                nc.gpsimd.tensor_scalar(out=o[:, i, :], in0=v[:], scalar1=rinv, scalar2=0.0, op0=ALU.mult, op1=ALU.add)

        def st(r, n):
            i = r % 2
            nc.sync.dma_start(out=out_v[:, r : r + n, :], in_=tiles["o_%d" % (r // 2)][:, i : i + n, :])

        ld_x(0, 1)
        ld_w1(0, 0)
        ld_x(1, 1)
        ld_w1(1, 0)
        ld_w1(0, 1)
        ld_w1(1, 1)
        ld_b()
        ld_x(2, 1)
        ld_x(3, 1)
        ld_x(4, 2)
        ld_w2(0)
        ld_w2(1)
        ld_x(6, 2)
        ld_b2()

        xt(0)
        xe(0, "S")
        for t in range(4):
            w1r(0, 0, t, "V")
        xt(1)
        xe(1, "S")
        w1q(0, 0)
        for t in range(2):
            w1r(1, 0, t, "V")
            w1r(1, 0, t + 2, "S")
        xq(0)
        w1q(1, 0)
        for t in range(2):
            w1r(0, 1, t, "S")
            w1r(0, 1, t + 2, "V")
        m1(0, 0, 0)
        m1(0, 1, 0)
        for t in range(4):
            w1r(1, 1, t, "V")
        he(0, 0, 0, "S")
        he(0, 1, 0, "S")
        w1q(0, 1)
        w1q(1, 1)
        xt(2)
        xt(3)
        xe(2, "S")
        xe(3, "S")
        m1(1, 0, 0)
        m1(1, 1, 0)
        xt(4)
        xt(5)
        hr(0, 0, "V")
        xq(1)
        he(1, 0, 0, "S")
        he(1, 1, 0, "S")
        xe(4, "S")
        w2r(0, 0, "V")
        xe(5, "S")
        m1(0, 0, 1)
        m1(0, 1, 1)
        m1(1, 0, 1)
        m1(1, 1, 1)
        hr(1, 0, "V")
        w2r(0, 1, "V")
        hq(0, 0, 2)
        xq(2)
        he(0, 0, 1, "S")
        he(0, 1, 1, "S")
        xt(6)
        xt(7)
        he(1, 0, 1, "S")
        he(1, 1, 1, "S")
        w2q(0)
        m1(0, 0, 2)
        m1(0, 1, 2)
        m1(1, 0, 2)
        m1(1, 1, 2)
        w2r(1, 0, "S")
        xe(6, "S")
        xe(7, "S")
        hr(0, 1, "V")
        hr(1, 1, "V")
        w2r(1, 1, "V")
        hq(1, 0, 2)
        w2q(1)
        he(0, 0, 2, "S")
        he(0, 1, 2, "S")
        xq(3)
        he(1, 0, 2, "S")
        he(1, 1, 2, "S")
        m2(0)
        m2(1)
        m1(0, 0, 3)
        m1(0, 1, 3)
        m1(1, 0, 3)
        m1(1, 1, 3)
        m2(2)
        m2(3)
        hr(0, 2, "V")
        he(0, 0, 3, "S")
        he(0, 1, 3, "S")
        va(0)
        hr(1, 2, "V")
        va(1)
        sq(0)
        he(1, 0, 3, "S")
        hq(2, 0, 2)
        hr(0, 3, "V")
        va(2)
        sq(1)
        he(1, 1, 3, "S")
        clamp(0)
        va(3)
        hq(3, 0, 1)
        hr(1, 3, "V")
        m2(4)
        m2(5)
        m2p(6, 0)
        m2p(7, 0)
        sq(2)
        rsq(0)
        sq(3)
        clamp(1)
        sc(0, "G")
        rsq(1)
        sc(1, "G")
        st(0, 2)
        va(4)
        hq(3, 1, 1)
        sc(2, "G")
        sc(3, "G")
        st(2, 2)
        m2p(6, 1)
        m2p(7, 1)
        sq(4)
        va(5)
        va(6)
        va(7)
        sq(5)
        clamp(2)
        rsq(2)
        sq(6)
        sq(7)
        clamp(3)
        rsq(3)
        sc(4, "V")
        sc(5, "V")
        st(4, 2)
        sc(6, "V")
        st(6, 1)
        sc(7, "V")
        st(7, 1)
